import numpy as np
import ml_dtypes


def mxq(x, axis, fmt="e4m3"):
    dtype, down = {"e4m3": (ml_dtypes.float8_e4m3fn, 7), "e5m2": (ml_dtypes.float8_e5m2, 14)}[fmt]
    v = np.moveaxis(np.asarray(x, np.float32).astype(ml_dtypes.bfloat16).astype(np.float64), axis, -1)
    blocks = v.reshape(v.shape[:-1] + (-1, 32))
    amax = np.abs(blocks).max(-1, keepdims=True)
    byte = np.maximum(np.where(amax > 0, np.frexp(amax)[1] - 1 + 127, 0) - down, 1)
    scale = np.exp2(byte - 127.0)
    codes = (blocks / scale).astype(np.float32).astype(dtype).astype(np.float64)
    return np.moveaxis((codes * scale).reshape(v.shape), -1, axis)


WIDE = False


def mx_kscale(k):
    if not WIDE:
        return np.ones(k)
    levels = np.array([18, -18])
    if k % 512:
        return np.exp2(np.random.permutation(np.resize(levels, k // 32))).repeat(32)
    a = np.empty((k // 512, 16))
    for p in range(k // 512):
        a[p, :8] = np.random.permutation(np.resize(levels, 8))
        for g in range(8):
            far = levels[np.abs(levels - a[p, g]) >= 10]
            a[p, g + 8] = far[np.random.randint(len(far))]
    return np.exp2(a.ravel()).repeat(32)


BF16 = ml_dtypes.bfloat16


def bf(x):
    return np.asarray(x, np.float32).astype(BF16)


def f64(x):
    return np.asarray(x).astype(np.float64)


B, EMBED, DETER, STOC, HID = 512, 1536, 1024, 256, 1024
DIST = 2 * STOC
CAT = DETER + EMBED


def softplus(v):
    return np.maximum(v, 0.0) + np.log(1.0 + np.exp(-np.abs(v)))


def sigmoid(v):
    return 1.0 / (1.0 + np.exp(-v))


def setup_inputs():
    s = mx_kscale(B)[:, None]
    u = mx_kscale(DIST)
    v = mx_kscale(HID)
    r = np.random.standard_normal
    h0 = bf(r((B, DETER)) * 0.65)
    e0 = bf(r((B, EMBED)))
    wp1 = bf(r((HID, DETER)) / np.sqrt(DETER))
    bp1 = bf(r(HID) * 0.1)
    wp2 = bf(r((DIST, HID)) / np.sqrt(HID))
    bp2 = bf(r(DIST) * 0.1)
    wq1_0 = bf(r((HID, CAT)) / np.sqrt(CAT))
    bq1 = bf(r(HID) * 0.1)
    wq2_0 = bf(r((DIST, HID)) / np.sqrt(HID))
    bq2 = bf(r(DIST) * 0.1)
    zq = np.concatenate([f64(h0), f64(e0)], -1) @ f64(wq1_0).T + f64(bq1)
    vq = (np.maximum(zq, 0.0) @ f64(wq2_0).T + f64(bq2))[:, STOC:]

    def grad():
        return r((B, STOC)) * np.exp2(np.random.randint(-6, 1, (B, 1))) * 4.0

    g0 = bf(grad() / s * u[:STOC])
    g1 = bf(grad() / s * u[STOC:])
    g2 = bf(grad())
    g3 = bf(grad())
    return {
        "h": bf(f64(h0) * s),
        "embedding": bf(f64(e0) * s),
        "wp1": wp1,
        "bp1": bp1,
        "wp2": wp2,
        "bp2": bp2,
        "wq1": bf(f64(wq1_0) / v[:, None]),
        "bq1": bq1,
        "wq2": bf(f64(wq2_0) / u[:, None] * v),
        "bq2": bq2,
        "zq": np.asarray(zq, np.float32),
        "vq": np.asarray(vq, np.float32),
        "grad_0": g0,
        "grad_1": g1,
        "grad_2": g2,
        "grad_3": g3,
    }


def reference(h, embedding, wp1, bp1, wp2, bp2, wq1, bq1, wq2, bq2, zq, vq, grad_0, grad_1, grad_2, grad_3):
    dz2 = np.concatenate([f64(grad_0), f64(grad_1) * sigmoid(f64(vq))], -1)
    da = mxq(dz2, 1, "e5m2") @ mxq(f64(wq2), 0, "e4m3")
    dz1 = np.where(f64(zq) > 0.0, da, 0.0)
    de = mxq(dz1, 1, "e5m2") @ mxq(f64(wq1)[:, DETER:], 0, "e4m3")
    c = np.concatenate([f64(h), f64(embedding)], -1)
    dwq1 = mxq(dz1, 0, "e5m2").T @ mxq(c, 0, "e4m3")
    return de, dwq1

@@ -1,0 +1,215 @@
+from contextlib import ExitStack
+
+import concourse.mybir as mybir
+from concourse.masks import make_identity
+
+B, EMBED, DETER, STOC, HID = 512, 1536, 1024, 256, 1024
+DIST = 2 * STOC
+
+FLOPS = 2 * (B * DIST * HID + B * HID * EMBED + HID * B * (DETER + EMBED))
+BYTES = 2 * (2 * B * STOC + DIST * HID + HID * EMBED + B * (DETER + EMBED)) + 4 * (B * STOC + B * HID) + 4 * (B * EMBED + HID * (DETER + EMBED))
+
+F32 = mybir.dt.float32
+BF16 = mybir.dt.bfloat16
+U32 = mybir.dt.uint32
+U8 = mybir.dt.uint8
+E4M3 = mybir.dt.float8_e4m3fn_x4
+E5M2 = mybir.dt.float8_e5m2_x4
+MULT = mybir.AluOpType.mult
+IS_GT = mybir.AluOpType.is_gt
+SIGMOID = mybir.ActivationFunctionType.Sigmoid
+
+P = 128
+PACK = 4
+COLS = 512
+VFROM = 6
+STAGED = {2: 6, 3: 6}
+
+
+def tile_rssmcell_pb_v_kernel(tc, h, embedding, wp1, bp1, wp2, bp2, wq1, bq1, wq2, bq2, zq, vq, grad_0, grad_1, grad_2, grad_3, out_0, out_1):
+    nc = tc.nc
+    with ExitStack() as ctx:
+        keep = ctx.enter_context(tc.tile_pool(name="keep", bufs=1))
+        grouping = ctx.enter_context(tc.tile_pool(name="grouping", bufs=8))
+        staging = ctx.enter_context(tc.tile_pool(name="staging", bufs=4))
+        psum = ctx.enter_context(tc.psum_pool(name="psum", bufs=8))
+        ctx.enter_context(tc.manual_schedule())
+
+        def rows4(ap):
+            return ap.rearrange("(p j) w -> p j w", j=PACK)
+
+        def operand(name):
+            codes = keep.tile([P, COLS], U32, name=name + "_codes", align_bytes=64)
+            scales = keep.tile([P, COLS], U8, name=name + "_scales", align_bytes=64)
+            return codes, scales
+
+        def new_grouped():
+            grouped = grouping.tile([P, COLS, PACK], BF16, name="grouped", align_bytes=64)
+            return grouped
+
+        def interleave(copy, rows):
+            grouped = new_grouped()
+            copy(out=grouped[:].rearrange("p (c i) t -> p c t i", i=4), in_=rows.rearrange("p t (c i) -> p c t i", i=4))
+            return grouped
+
+        def quantize(target, grouped, fmt):
+            codes, scales = target
+            nc.vector.quantize_mx(out=codes[:].bitcast(fmt), scales=scales[:], in_=grouped[:].rearrange("p w t -> p (w t)"))
+
+        def transpose_pair(rows, pair):
+            bank = psum.tile([P, COLS], F32, name="bank")
+            for jj in range(2):
+                words = rows[:, 2 * pair + jj, :].bitcast(F32)
+                for u in range(2):
+                    at = P * (2 * jj + u)
+                    nc.tensor.transpose(bank[:, at : at + P], words[:, u::2], ident[:])
+            return bank
+
+        def gather_pair(copy, grouped, pair, bank):
+            words = grouped[:].rearrange("p w t -> p (w t)").bitcast(F32)
+            copy(out=words[:, COLS * pair : COLS * (pair + 1)].rearrange("p (j r u) -> p j r u", j=2, u=2), in_=bank[:].rearrange("p (j u r) -> p j r u", j=2, u=2))
+
+        def mx(bank, stationary, m, moving, start, stop):
+            cols = slice(P * m, P * (m + 1))
+            nc.tensor.matmul_mx(
+                out=bank[:],
+                lhsT=stationary[0][:, cols].bitcast(E5M2),
+                lhsT_scale=stationary[1][:, cols],
+                rhs=moving[0][:].bitcast(E4M3),
+                rhs_scale=moving[1][:],
+                start=start,
+                stop=stop,
+            )
+
+        vcopy, scopy = nc.vector.tensor_copy, nc.scalar.copy
+
+        v_raw = keep.tile([P, PACK, STOC], F32, name="v_raw")
+        nc.sync.dma_start(out=v_raw[:], in_=rows4(vq))
+        g1_raw = keep.tile([P, PACK, STOC], BF16, name="g1_raw")
+        nc.sync.dma_start(out=g1_raw[:], in_=rows4(grad_1))
+        dz2 = keep.tile([P, PACK, DIST], BF16, name="dz2")
+        nc.sync.dma_start(out=dz2[:, :, 0:STOC], in_=rows4(grad_0))
+        wq2_raw = keep.tile([P, PACK, HID], BF16, name="wq2_raw")
+        nc.sync.dma_start(out=wq2_raw[:], in_=rows4(wq2))
+        h_raw = keep.tile([P, PACK, DETER], BF16, name="h_raw")
+        nc.sync.dma_start(out=h_raw[:], in_=rows4(h))
+        z_raw = []
+        for g in range(2):
+            z = keep.tile([P, PACK, COLS], F32, name="z_raw%d" % g)
+            nc.sync.dma_start(out=z[:], in_=rows4(zq)[:, :, COLS * g : COLS * (g + 1)])
+            z_raw.append(z)
+        e_raw = keep.tile([P, PACK, EMBED], BF16, name="e_raw")
+        nc.sync.dma_start(out=e_raw[:], in_=rows4(embedding))
+        w_raw = []
+        for g in range(2):
+            w = keep.tile([P, PACK, EMBED], BF16, name="w_raw%d" % g)
+            nc.sync.dma_start(out=w[:], in_=rows4(wq1[COLS * g : COLS * (g + 1), DETER:]))
+            w_raw.append(w)
+
+        ident = keep.tile([P, P], F32, name="ident")
+        make_identity(nc, ident[:])
+
+        sig = keep.tile([P, PACK, STOC], F32, name="sig")
+        for pair in range(2):
+            js = slice(2 * pair, 2 * pair + 2)
+            nc.scalar.activation(out=sig[:, js, :], in_=v_raw[:, js, :], func=SIGMOID)
+            nc.vector.tensor_tensor(out=dz2[:, js, STOC:], in0=g1_raw[:, js, :], in1=sig[:, js, :], op=MULT)
+        banks = [transpose_pair(dz2, pair) for pair in range(2)]
+        w2_grouped = [interleave(vcopy, wq2_raw[:, :, 0:COLS])]
+        dz2_grouped = new_grouped()
+        for pair in range(2):
+            gather_pair(scopy, dz2_grouped, pair, banks[pair])
+        w2_op = [operand("w2_0"), operand("w2_1")]
+        quantize(w2_op[0], w2_grouped[0], E4M3)
+        dz2_op = operand("dz2")
+        quantize(dz2_op, dz2_grouped, E5M2)
+        w2_grouped.append(interleave(scopy, wq2_raw[:, :, COLS:]))
+
+        def da_banks(g):
+            banks = []
+            for j in range(PACK):
+                bank = psum.tile([P, COLS], F32, name="bank")
+                mx(bank, dz2_op, j, w2_op[g], True, True)
+                banks.append(bank)
+            return banks
+
+        dz1 = []
+        dz1_tok = [operand("dz1_tok%d" % g) for g in range(2)]
+        dz1_hid = [operand("dz1_hid%d" % g) for g in range(2)]
+
+        def mask(g, banks):
+            rows = keep.tile([P, PACK, COLS], BF16, name="dz1_rows%d" % g)
+            for j in range(PACK):
+                nc.vector.scalar_tensor_tensor(out=rows[:, j, :], in0=z_raw[g][:, j, :], scalar=0.0, in1=banks[j][:], op0=IS_GT, op1=MULT)
+            dz1.append(rows)
+
+        c_op = [operand("c%d" % n) for n in range(5)]
+        w1_op = [[operand("w1_%d_%d" % (g, n)) for n in range(3)] for g in range(2)]
+
+        da0 = da_banks(0)
+        h_grouped = [interleave(scopy, h_raw[:, :, 0:COLS])]
+        quantize(w2_op[1], w2_grouped[1], E4M3)
+        da1 = da_banks(1)
+        h_grouped.append(interleave(vcopy, h_raw[:, :, COLS:]))
+        mask(0, da0)
+        quantize(c_op[0], h_grouped[0], E4M3)
+        tok_grouped = interleave(vcopy, dz1[0][:])
+        quantize(c_op[1], h_grouped[1], E4M3)
+        quantize(dz1_tok[0], tok_grouped, E5M2)
+        mask(1, da1)
+        hid_grouped = [new_grouped(), new_grouped()]
+        banks = [transpose_pair(dz1[0], pair) for pair in range(2)]
+        for pair in range(2):
+            gather_pair(scopy, hid_grouped[0], pair, banks[pair])
+        tok_grouped = interleave(vcopy, dz1[1][:])
+
+        def evacuate(copy, out, bank):
+            copy(out=out, in_=bank[:])
+
+        def out1_tile(m, first, count, copies):
+            staged = staging.tile([P, count * COLS], F32, name="staged%d" % count, bufs=STAGED[count])
+            for n in range(count):
+                bank = psum.tile([P, COLS], F32, name="bank")
+                mx(bank, dz1_tok[m // 4], m % 4, c_op[first + n], True, True)
+                evacuate(copies[n], staged[:, COLS * n : COLS * (n + 1)], bank)
+            nc.sync.dma_start(out=out_1[P * m : P * (m + 1), COLS * first : COLS * (first + count)], in_=staged[:])
+
+        out1_tile(0, 0, 2, (scopy, scopy))
+        quantize(dz1_tok[1], tok_grouped, E5M2)
+        out1_tile(1, 0, 2, (scopy, scopy))
+        quantize(dz1_hid[0], hid_grouped[0], E5M2)
+        banks = [transpose_pair(dz1[1], pair) for pair in range(2)]
+        for pair in range(2):
+            gather_pair(scopy, hid_grouped[1], pair, banks[pair])
+        e_grouped = [interleave(vcopy, e_raw[:, :, COLS * n : COLS * (n + 1)]) for n in range(2)]
+        out1_tile(2, 0, 2, (scopy, scopy))
+        quantize(c_op[2], e_grouped[0], E4M3)
+        e_grouped.append(interleave(vcopy, e_raw[:, :, 2 * COLS :]))
+        quantize(c_op[3], e_grouped[1], E4M3)
+        quantize(dz1_hid[1], hid_grouped[1], E5M2)
+        quantize(c_op[4], e_grouped[2], E4M3)
+        for m in range(3, 8):
+            out1_tile(m, 0, 2, (scopy, scopy))
+
+        chunks = [(g, n) for n in range(3) for g in range(2)]
+        w_grouped = []
+        for m in range(8):
+            if m < 6:
+                g, n = chunks[m]
+                w_grouped.append(interleave(vcopy, w_raw[g][:, :, COLS * n : COLS * (n + 1)]))
+            out1_tile(m, 2, 3, (scopy, vcopy if m > VFROM else scopy, scopy))
+            if m >= 1 and m < 7:
+                g, n = chunks[m - 1]
+                quantize(w1_op[g][n], w_grouped[m - 1], E4M3)
+
+        for j in range(PACK):
+            staged = staging.tile([P, EMBED], F32, name="staged3", bufs=STAGED[3])
+            for n in range(3):
+                bank = psum.tile([P, COLS], F32, name="bank")
+                for g in range(2):
+                    mx(bank, dz1_hid[g], j, w1_op[g][n], g == 0, g == 1)
+                evacuate((scopy, vcopy)[(3 * j + n) % 2], staged[:, COLS * n : COLS * (n + 1)], bank)
+                if j == 3:
+                    nc.sync.dma_start(out=rows4(out_0)[:, j, COLS * n : COLS * (n + 1)], in_=staged[:, COLS * n : COLS * (n + 1)])
+            if j < 3:
+                nc.sync.dma_start(out=rows4(out_0)[:, j, :], in_=staged[:])

@@ -23,14 +23,14 @@ P = 128
 PACK = 4
 COLS = 512
 VFROM = 6
-STAGED = {2: 6, 3: 6}
+STAGED = {2: 5, 3: 4}
 
 
 def tile_rssmcell_pb_v_kernel(tc, h, embedding, wp1, bp1, wp2, bp2, wq1, bq1, wq2, bq2, zq, vq, grad_0, grad_1, grad_2, grad_3, out_0, out_1):
     nc = tc.nc
     with ExitStack() as ctx:
         keep = ctx.enter_context(tc.tile_pool(name="keep", bufs=1))
-        grouping = ctx.enter_context(tc.tile_pool(name="grouping", bufs=8))
+        grouping = ctx.enter_context(tc.tile_pool(name="grouping", bufs=6))
         staging = ctx.enter_context(tc.tile_pool(name="staging", bufs=4))
         psum = ctx.enter_context(tc.psum_pool(name="psum", bufs=8))
         ctx.enter_context(tc.manual_schedule())
@@ -85,18 +85,19 @@ def tile_rssmcell_pb_v_kernel(tc, h, embedding, wp1, bp1, wp2, bp2, wq1, bq1, wq
 
         v_raw = keep.tile([P, PACK, STOC], F32, name="v_raw")
         nc.sync.dma_start(out=v_raw[:], in_=rows4(vq))
+        g0_raw = keep.tile([P, PACK, STOC], BF16, name="g0_raw")
+        nc.sync.dma_start(out=g0_raw[:], in_=rows4(grad_0))
         g1_raw = keep.tile([P, PACK, STOC], BF16, name="g1_raw")
         nc.sync.dma_start(out=g1_raw[:], in_=rows4(grad_1))
         dz2 = keep.tile([P, PACK, DIST], BF16, name="dz2")
-        nc.sync.dma_start(out=dz2[:, :, 0:STOC], in_=rows4(grad_0))
         wq2_raw = keep.tile([P, PACK, HID], BF16, name="wq2_raw")
         nc.sync.dma_start(out=wq2_raw[:], in_=rows4(wq2))
         h_raw = keep.tile([P, PACK, DETER], BF16, name="h_raw")
         nc.sync.dma_start(out=h_raw[:], in_=rows4(h))
         z_raw = []
-        for g in range(2):
-            z = keep.tile([P, PACK, COLS], F32, name="z_raw%d" % g)
-            nc.sync.dma_start(out=z[:], in_=rows4(zq)[:, :, COLS * g : COLS * (g + 1)])
+        for pair in range(2):
+            z = keep.tile([P, 2, HID], F32, name="z_raw%d" % pair)
+            nc.sync.dma_start(out=z[:], in_=rows4(zq)[:, 2 * pair : 2 * pair + 2, :])
             z_raw.append(z)
         e_raw = keep.tile([P, PACK, EMBED], BF16, name="e_raw")
         nc.sync.dma_start(out=e_raw[:], in_=rows4(embedding))
@@ -110,6 +111,7 @@ def tile_rssmcell_pb_v_kernel(tc, h, embedding, wp1, bp1, wp2, bp2, wq1, bq1, wq
         make_identity(nc, ident[:])
 
         sig = keep.tile([P, PACK, STOC], F32, name="sig")
+        vcopy(out=dz2[:, :, 0:STOC], in_=g0_raw[:])
         for pair in range(2):
             js = slice(2 * pair, 2 * pair + 2)
             nc.scalar.activation(out=sig[:, js, :], in_=v_raw[:, js, :], func=SIGMOID)
@@ -125,43 +127,45 @@ def tile_rssmcell_pb_v_kernel(tc, h, embedding, wp1, bp1, wp2, bp2, wq1, bq1, wq
         quantize(dz2_op, dz2_grouped, E5M2)
         w2_grouped.append(interleave(scopy, wq2_raw[:, :, COLS:]))
 
-        def da_banks(g):
+        dz1_tok = [operand("dz1_tok%d" % g) for g in range(2)]
+        dz1_hid = [operand("dz1_hid%d" % g) for g in range(2)]
+        c_op = [operand("c%d" % n) for n in range(5)]
+        w1_op = [[operand("w1_%d_%d" % (g, n)) for n in range(3)] for g in range(2)]
+        dz1 = [keep.tile([P, PACK, COLS], BF16, name="dz1_%d" % g) for g in range(2)]
+
+        def da_banks(g, pair):
             banks = []
-            for j in range(PACK):
+            for j in (2 * pair, 2 * pair + 1):
                 bank = psum.tile([P, COLS], F32, name="bank")
                 mx(bank, dz2_op, j, w2_op[g], True, True)
                 banks.append(bank)
             return banks
 
-        dz1 = []
-        dz1_tok = [operand("dz1_tok%d" % g) for g in range(2)]
-        dz1_hid = [operand("dz1_hid%d" % g) for g in range(2)]
+        def mask(g, pair, banks):
+            for jj in range(2):
+                nc.vector.scalar_tensor_tensor(out=dz1[g][:, 2 * pair + jj, :], in0=z_raw[pair][:, jj, COLS * g : COLS * (g + 1)], scalar=0.0, in1=banks[jj][:], op0=IS_GT, op1=MULT)
 
-        def mask(g, banks):
-            rows = keep.tile([P, PACK, COLS], BF16, name="dz1_rows%d" % g)
-            for j in range(PACK):
-                nc.vector.scalar_tensor_tensor(out=rows[:, j, :], in0=z_raw[g][:, j, :], scalar=0.0, in1=banks[j][:], op0=IS_GT, op1=MULT)
-            dz1.append(rows)
-
-        c_op = [operand("c%d" % n) for n in range(5)]
-        w1_op = [[operand("w1_%d_%d" % (g, n)) for n in range(3)] for g in range(2)]
-
-        da0 = da_banks(0)
-        h_grouped = [interleave(scopy, h_raw[:, :, 0:COLS])]
+        da = [[da_banks(0, 0)], []]
         quantize(w2_op[1], w2_grouped[1], E4M3)
-        da1 = da_banks(1)
-        h_grouped.append(interleave(vcopy, h_raw[:, :, COLS:]))
-        mask(0, da0)
-        quantize(c_op[0], h_grouped[0], E4M3)
-        tok_grouped = interleave(vcopy, dz1[0][:])
-        quantize(c_op[1], h_grouped[1], E4M3)
-        quantize(dz1_tok[0], tok_grouped, E5M2)
-        mask(1, da1)
+        da[1].append(da_banks(1, 0))
+        da[0].append(da_banks(0, 1))
+        da[1].append(da_banks(1, 1))
+        h_grouped = [interleave(scopy, h_raw[:, :, 0:COLS]), interleave(vcopy, h_raw[:, :, COLS:])]
+        mask(0, 0, da[0][0])
+        mask(1, 0, da[1][0])
         hid_grouped = [new_grouped(), new_grouped()]
-        banks = [transpose_pair(dz1[0], pair) for pair in range(2)]
-        for pair in range(2):
-            gather_pair(scopy, hid_grouped[0], pair, banks[pair])
-        tok_grouped = interleave(vcopy, dz1[1][:])
+        for g in range(2):
+            bank = transpose_pair(dz1[g], 0)
+            gather_pair(scopy, hid_grouped[g], 0, bank)
+        mask(0, 1, da[0][1])
+        tok_grouped = [interleave(vcopy, dz1[0][:])]
+        quantize(c_op[0], h_grouped[0], E4M3)
+        quantize(dz1_tok[0], tok_grouped[0], E5M2)
+        bank = transpose_pair(dz1[0], 1)
+        gather_pair(scopy, hid_grouped[0], 1, bank)
+        quantize(c_op[1], h_grouped[1], E4M3)
+        mask(1, 1, da[1][1])
+        tok_grouped.append(interleave(vcopy, dz1[1][:]))
 
         def evacuate(copy, out, bank):
             copy(out=out, in_=bank[:])
@@ -174,42 +178,40 @@ def tile_rssmcell_pb_v_kernel(tc, h, embedding, wp1, bp1, wp2, bp2, wq1, bq1, wq
                 evacuate(copies[n], staged[:, COLS * n : COLS * (n + 1)], bank)
             nc.sync.dma_start(out=out_1[P * m : P * (m + 1), COLS * first : COLS * (first + count)], in_=staged[:])
 
-        out1_tile(0, 0, 2, (scopy, scopy))
-        quantize(dz1_tok[1], tok_grouped, E5M2)
-        out1_tile(1, 0, 2, (scopy, scopy))
-        quantize(dz1_hid[0], hid_grouped[0], E5M2)
-        banks = [transpose_pair(dz1[1], pair) for pair in range(2)]
-        for pair in range(2):
-            gather_pair(scopy, hid_grouped[1], pair, banks[pair])
-        e_grouped = [interleave(vcopy, e_raw[:, :, COLS * n : COLS * (n + 1)]) for n in range(2)]
-        out1_tile(2, 0, 2, (scopy, scopy))
+        split = 8
+        e_grouped = []
+        for m in range(split):
+            if m == 2:
+                e_grouped.append(interleave(vcopy, e_raw[:, :, 0:COLS]))
+                quantize(dz1_tok[1], tok_grouped[1], E5M2)
+            out1_tile(m, 0, 2, (scopy,) * 2)
+            if m == 1:
+                bank = transpose_pair(dz1[1], 1)
+                gather_pair(scopy, hid_grouped[1], 1, bank)
+        e_grouped.append(interleave(vcopy, e_raw[:, :, COLS : 2 * COLS]))
         quantize(c_op[2], e_grouped[0], E4M3)
         e_grouped.append(interleave(vcopy, e_raw[:, :, 2 * COLS :]))
         quantize(c_op[3], e_grouped[1], E4M3)
-        quantize(dz1_hid[1], hid_grouped[1], E5M2)
+        quantize(dz1_hid[0], hid_grouped[0], E5M2)
         quantize(c_op[4], e_grouped[2], E4M3)
-        for m in range(3, 8):
-            out1_tile(m, 0, 2, (scopy, scopy))
-
+        quantize(dz1_hid[1], hid_grouped[1], E5M2)
         chunks = [(g, n) for n in range(3) for g in range(2)]
         w_grouped = []
         for m in range(8):
             if m < 6:
                 g, n = chunks[m]
                 w_grouped.append(interleave(vcopy, w_raw[g][:, :, COLS * n : COLS * (n + 1)]))
-            out1_tile(m, 2, 3, (scopy, vcopy if m > VFROM else scopy, scopy))
+            out1_tile(m, 2, 3, (scopy, vcopy, scopy) if m > 6 else (scopy,) * 3)
             if m >= 1 and m < 7:
                 g, n = chunks[m - 1]
                 quantize(w1_op[g][n], w_grouped[m - 1], E4M3)
 
-        for j in range(PACK):
-            staged = staging.tile([P, EMBED], F32, name="staged3", bufs=STAGED[3])
-            for n in range(3):
-                bank = psum.tile([P, COLS], F32, name="bank")
-                for g in range(2):
-                    mx(bank, dz1_hid[g], j, w1_op[g][n], g == 0, g == 1)
-                evacuate((scopy, vcopy)[(3 * j + n) % 2], staged[:, COLS * n : COLS * (n + 1)], bank)
-                if j == 3:
-                    nc.sync.dma_start(out=rows4(out_0)[:, j, COLS * n : COLS * (n + 1)], in_=staged[:, COLS * n : COLS * (n + 1)])
-            if j < 3:
-                nc.sync.dma_start(out=rows4(out_0)[:, j, :], in_=staged[:])
+        for pair in range(2):
+            staged = staging.tile([P, 2, EMBED], F32, name="staged_out0", bufs=2)
+            for jj in range(2):
+                for n in range(3):
+                    bank = psum.tile([P, COLS], F32, name="bank")
+                    for g in range(2):
+                        mx(bank, dz1_hid[g], 2 * pair + jj, w1_op[g][n], g == 0, g == 1)
+                    evacuate((scopy, vcopy)[n % 2], staged[:, jj, COLS * n : COLS * (n + 1)], bank)
+            nc.sync.dma_start(out=rows4(out_0)[:, 2 * pair : 2 * pair + 2, :], in_=staged[:])

@@ -150,7 +150,7 @@ def tile_rssmcell_pb_v_kernel(tc, h, embedding, wp1, bp1, wp2, bp2, wq1, bq1, wq
         da[1].append(da_banks(1, 0))
         da[0].append(da_banks(0, 1))
         da[1].append(da_banks(1, 1))
-        h_grouped = [interleave(scopy, h_raw[:, :, 0:COLS]), interleave(vcopy, h_raw[:, :, COLS:])]
+        h_grouped = [interleave(scopy, h_raw[:, :, 0:COLS]), interleave(scopy, h_raw[:, :, COLS:])]
         mask(0, 0, da[0][0])
         mask(1, 0, da[1][0])
         hid_grouped = [new_grouped(), new_grouped()]

from contextlib import ExitStack

import concourse.mybir as mybir
from concourse.masks import make_identity

B, EMBED, DETER, STOC, HID = 512, 1536, 1024, 256, 1024
DIST = 2 * STOC

FLOPS = 2 * (B * DIST * HID + B * HID * EMBED + HID * B * (DETER + EMBED))
BYTES = 2 * (2 * B * STOC + DIST * HID + HID * EMBED + B * (DETER + EMBED)) + 4 * (B * STOC + B * HID) + 4 * (B * EMBED + HID * (DETER + EMBED))

F32 = mybir.dt.float32
BF16 = mybir.dt.bfloat16
U32 = mybir.dt.uint32
U8 = mybir.dt.uint8
E4M3 = mybir.dt.float8_e4m3fn_x4
E5M2 = mybir.dt.float8_e5m2_x4
MULT = mybir.AluOpType.mult
IS_GT = mybir.AluOpType.is_gt
SIGMOID = mybir.ActivationFunctionType.Sigmoid

P = 128
PACK = 4
COLS = 512
VFROM = 6
STAGED = {2: 5, 3: 4}


def tile_rssmcell_pb_v_kernel(tc, h, embedding, wp1, bp1, wp2, bp2, wq1, bq1, wq2, bq2, zq, vq, grad_0, grad_1, grad_2, grad_3, out_0, out_1):
    nc = tc.nc
    with ExitStack() as ctx:
        keep = ctx.enter_context(tc.tile_pool(name="keep", bufs=1))
        grouping = ctx.enter_context(tc.tile_pool(name="grouping", bufs=6))
        staging = ctx.enter_context(tc.tile_pool(name="staging", bufs=4))
        psum = ctx.enter_context(tc.psum_pool(name="psum", bufs=8))
        ctx.enter_context(tc.manual_schedule())

        def rows4(ap):
            return ap.rearrange("(p j) w -> p j w", j=PACK)

        def operand(name):
            codes = keep.tile([P, COLS], U32, name=name + "_codes", align_bytes=64)
            scales = keep.tile([P, COLS], U8, name=name + "_scales", align_bytes=64)
            return codes, scales

        def new_grouped():
            grouped = grouping.tile([P, COLS, PACK], BF16, name="grouped", align_bytes=64)
            return grouped

        def interleave(copy, rows):
            grouped = new_grouped()
            copy(out=grouped[:].rearrange("p (c i) t -> p c t i", i=4), in_=rows.rearrange("p t (c i) -> p c t i", i=4))
            return grouped

        def quantize(target, grouped, fmt):
            codes, scales = target
            nc.vector.quantize_mx(out=codes[:].bitcast(fmt), scales=scales[:], in_=grouped[:].rearrange("p w t -> p (w t)"))

        def transpose_pair(rows, pair):
            bank = psum.tile([P, COLS], F32, name="bank")
            for jj in range(2):
                words = rows[:, 2 * pair + jj, :].bitcast(F32)
                for u in range(2):
                    at = P * (2 * jj + u)
                    nc.tensor.transpose(bank[:, at : at + P], words[:, u::2], ident[:])
            return bank

        def gather_pair(copy, grouped, pair, bank):
            words = grouped[:].rearrange("p w t -> p (w t)").bitcast(F32)
            copy(out=words[:, COLS * pair : COLS * (pair + 1)].rearrange("p (j r u) -> p j r u", j=2, u=2), in_=bank[:].rearrange("p (j u r) -> p j r u", j=2, u=2))

        def mx(bank, stationary, m, moving, start, stop):
            cols = slice(P * m, P * (m + 1))
            nc.tensor.matmul_mx(
                out=bank[:],
                lhsT=stationary[0][:, cols].bitcast(E5M2),
                lhsT_scale=stationary[1][:, cols],
                rhs=moving[0][:].bitcast(E4M3),
                rhs_scale=moving[1][:],
                start=start,
                stop=stop,
            )

        vcopy, scopy = nc.vector.tensor_copy, nc.scalar.copy

        v_raw = keep.tile([P, PACK, STOC], F32, name="v_raw")
        nc.sync.dma_start(out=v_raw[:], in_=rows4(vq))
        g0_raw = keep.tile([P, PACK, STOC], BF16, name="g0_raw")
        nc.sync.dma_start(out=g0_raw[:], in_=rows4(grad_0))
        g1_raw = keep.tile([P, PACK, STOC], BF16, name="g1_raw")
        nc.sync.dma_start(out=g1_raw[:], in_=rows4(grad_1))
        dz2 = keep.tile([P, PACK, DIST], BF16, name="dz2")
        wq2_raw = keep.tile([P, PACK, HID], BF16, name="wq2_raw")
        nc.sync.dma_start(out=wq2_raw[:], in_=rows4(wq2))
        h_raw = keep.tile([P, PACK, DETER], BF16, name="h_raw")
        nc.sync.dma_start(out=h_raw[:], in_=rows4(h))
        z_raw = []
        for pair in range(2):
            z = keep.tile([P, 2, HID], F32, name="z_raw%d" % pair)
            nc.sync.dma_start(out=z[:], in_=rows4(zq)[:, 2 * pair : 2 * pair + 2, :])
            z_raw.append(z)
        e_raw = keep.tile([P, PACK, EMBED], BF16, name="e_raw")
        nc.sync.dma_start(out=e_raw[:], in_=rows4(embedding))
        w_raw = []
        for g in range(2):
            w = keep.tile([P, PACK, EMBED], BF16, name="w_raw%d" % g)
            nc.sync.dma_start(out=w[:], in_=rows4(wq1[COLS * g : COLS * (g + 1), DETER:]))
            w_raw.append(w)

        ident = keep.tile([P, P], F32, name="ident")
        make_identity(nc, ident[:])

        sig = keep.tile([P, PACK, STOC], F32, name="sig")
        vcopy(out=dz2[:, :, 0:STOC], in_=g0_raw[:])
        for pair in range(2):
            js = slice(2 * pair, 2 * pair + 2)
            nc.scalar.activation(out=sig[:, js, :], in_=v_raw[:, js, :], func=SIGMOID)
            nc.vector.tensor_tensor(out=dz2[:, js, STOC:], in0=g1_raw[:, js, :], in1=sig[:, js, :], op=MULT)
        banks = [transpose_pair(dz2, pair) for pair in range(2)]
        w2_grouped = [interleave(vcopy, wq2_raw[:, :, 0:COLS])]
        dz2_grouped = new_grouped()
        for pair in range(2):
            gather_pair(scopy, dz2_grouped, pair, banks[pair])
        w2_op = [operand("w2_0"), operand("w2_1")]
        quantize(w2_op[0], w2_grouped[0], E4M3)
        dz2_op = operand("dz2")
        quantize(dz2_op, dz2_grouped, E5M2)
        w2_grouped.append(interleave(scopy, wq2_raw[:, :, COLS:]))

        dz1_tok = [operand("dz1_tok%d" % g) for g in range(2)]
        dz1_hid = [operand("dz1_hid%d" % g) for g in range(2)]
        c_op = [operand("c%d" % n) for n in range(5)]
        w1_op = [[operand("w1_%d_%d" % (g, n)) for n in range(3)] for g in range(2)]
        dz1 = [keep.tile([P, PACK, COLS], BF16, name="dz1_%d" % g) for g in range(2)]

        def da_banks(g, pair):
            banks = []
            for j in (2 * pair, 2 * pair + 1):
                bank = psum.tile([P, COLS], F32, name="bank")
                mx(bank, dz2_op, j, w2_op[g], True, True)
                banks.append(bank)
            return banks

        def mask(g, pair, banks):
            for jj in range(2):
                nc.vector.scalar_tensor_tensor(out=dz1[g][:, 2 * pair + jj, :], in0=z_raw[pair][:, jj, COLS * g : COLS * (g + 1)], scalar=0.0, in1=banks[jj][:], op0=IS_GT, op1=MULT)

        da = [[da_banks(0, 0)], []]
        quantize(w2_op[1], w2_grouped[1], E4M3)
        da[1].append(da_banks(1, 0))
        da[0].append(da_banks(0, 1))
        da[1].append(da_banks(1, 1))
        h_grouped = [interleave(scopy, h_raw[:, :, 0:COLS]), interleave(scopy, h_raw[:, :, COLS:])]
        mask(0, 0, da[0][0])
        mask(1, 0, da[1][0])
        hid_grouped = [new_grouped(), new_grouped()]
        for g in range(2):
            bank = transpose_pair(dz1[g], 0)
            gather_pair(scopy, hid_grouped[g], 0, bank)
        mask(0, 1, da[0][1])
        tok_grouped = [interleave(vcopy, dz1[0][:])]
        quantize(c_op[0], h_grouped[0], E4M3)
        quantize(dz1_tok[0], tok_grouped[0], E5M2)
        bank = transpose_pair(dz1[0], 1)
        gather_pair(scopy, hid_grouped[0], 1, bank)
        quantize(c_op[1], h_grouped[1], E4M3)
        mask(1, 1, da[1][1])
        tok_grouped.append(interleave(vcopy, dz1[1][:]))

        def evacuate(copy, out, bank):
            copy(out=out, in_=bank[:])

        def out1_tile(m, first, count, copies):
            staged = staging.tile([P, count * COLS], F32, name="staged%d" % count, bufs=STAGED[count])
            for n in range(count):
                bank = psum.tile([P, COLS], F32, name="bank")
                mx(bank, dz1_tok[m // 4], m % 4, c_op[first + n], True, True)
                evacuate(copies[n], staged[:, COLS * n : COLS * (n + 1)], bank)
            nc.sync.dma_start(out=out_1[P * m : P * (m + 1), COLS * first : COLS * (first + count)], in_=staged[:])

        split = 8
        e_grouped = []
        for m in range(split):
            if m == 2:
                e_grouped.append(interleave(vcopy, e_raw[:, :, 0:COLS]))
                quantize(dz1_tok[1], tok_grouped[1], E5M2)
            out1_tile(m, 0, 2, (scopy,) * 2)
            if m == 1:
                bank = transpose_pair(dz1[1], 1)
                gather_pair(scopy, hid_grouped[1], 1, bank)
        e_grouped.append(interleave(vcopy, e_raw[:, :, COLS : 2 * COLS]))
        quantize(c_op[2], e_grouped[0], E4M3)
        e_grouped.append(interleave(vcopy, e_raw[:, :, 2 * COLS :]))
        quantize(c_op[3], e_grouped[1], E4M3)
        quantize(dz1_hid[0], hid_grouped[0], E5M2)
        quantize(c_op[4], e_grouped[2], E4M3)
        quantize(dz1_hid[1], hid_grouped[1], E5M2)
        chunks = [(g, n) for n in range(3) for g in range(2)]
        w_grouped = []
        for m in range(8):
            if m < 6:
                g, n = chunks[m]
                w_grouped.append(interleave(vcopy, w_raw[g][:, :, COLS * n : COLS * (n + 1)]))
            out1_tile(m, 2, 3, (scopy, vcopy, scopy) if m > 6 else (scopy,) * 3)
            if m >= 1 and m < 7:
                g, n = chunks[m - 1]
                quantize(w1_op[g][n], w_grouped[m - 1], E4M3)

        for pair in range(2):
            staged = staging.tile([P, 2, EMBED], F32, name="staged_out0", bufs=2)
            for jj in range(2):
                for n in range(3):
                    bank = psum.tile([P, COLS], F32, name="bank")
                    for g in range(2):
                        mx(bank, dz1_hid[g], 2 * pair + jj, w1_op[g][n], g == 0, g == 1)
                    evacuate((scopy, vcopy)[n % 2], staged[:, jj, COLS * n : COLS * (n + 1)], bank)
            nc.sync.dma_start(out=rows4(out_0)[:, 2 * pair : 2 * pair + 2, :], in_=staged[:])
